import numpy as np
import ml_dtypes


def mxq(x, axis, fmt="e4m3"):
    dtype, down = {"e4m3": (ml_dtypes.float8_e4m3fn, 7), "e5m2": (ml_dtypes.float8_e5m2, 14)}[fmt]
    v = np.moveaxis(np.asarray(x, np.float32).astype(ml_dtypes.bfloat16).astype(np.float64), axis, -1)
    blocks = v.reshape(v.shape[:-1] + (-1, 32))
    amax = np.abs(blocks).max(-1, keepdims=True)
    byte = np.maximum(np.where(amax > 0, np.frexp(amax)[1] - 1 + 127, 0) - down, 1)
    scale = np.exp2(byte - 127.0)
    codes = (blocks / scale).astype(np.float32).astype(dtype).astype(np.float64)
    return np.moveaxis((codes * scale).reshape(v.shape), -1, axis)


WIDE = False


def mx_kscale(k):
    if not WIDE:
        return np.ones(k)
    levels = np.array([10, -10, 5, -5, 0])
    if k % 512:
        return np.exp2(np.random.permutation(np.resize(levels, k // 32))).repeat(32)
    a = np.empty((k // 512, 16))
    for p in range(k // 512):
        a[p, :8] = np.random.permutation(np.resize(levels, 8))
        for g in range(8):
            far = levels[np.abs(levels - a[p, g]) >= 10]
            a[p, g + 8] = far[np.random.randint(len(far))]
    return np.exp2(a.ravel()).repeat(32)


BF16 = ml_dtypes.bfloat16


def bf(x):
    return np.asarray(x, np.float32).astype(BF16)


def f64(x):
    return np.asarray(x).astype(np.float64)


B, I, H = 1024, 2048, 256


def sigmoid(v):
    return 1.0 / (1.0 + np.exp(-v))


def setup_inputs():
    s = mx_kscale(I)
    return {
        "input_": bf(np.random.standard_normal((B, I)) * s),
        "c_input": bf(np.random.standard_normal((B, 1, H))),
        "h_0": bf(np.random.standard_normal((B, H))),
        "weight_ih": bf(np.random.standard_normal((I, 3 * H)) / np.sqrt(I) / s[:, None]),
        "weight_hh": bf(np.random.standard_normal((H, 3 * H)) / np.sqrt(H)),
        "alpha_weight_ih": bf(np.random.standard_normal((I, H)) / np.sqrt(I) / s[:, None]),
        "alpha_weight_hh": bf(np.random.standard_normal((H, H)) / np.sqrt(H)),
        "bias": bf(np.random.standard_normal(3 * H) * 0.5),
        "alpha_bias": bf(np.random.standard_normal(H) * 0.5),
    }


def reference(input_, c_input, h_0, weight_ih, weight_hh, alpha_weight_ih, alpha_weight_hh, bias, alpha_bias):
    xq = mxq(f64(input_), 1, "e4m3")
    wh_b = f64(h_0) @ f64(weight_hh) + f64(bias)
    wi = xq @ mxq(f64(weight_ih), 0, "e4m3")
    pre = wh_b + wi
    i_gate = sigmoid(pre[:, :H])
    o_gate = sigmoid(pre[:, H:2 * H])
    g = np.tanh(pre[:, 2 * H:])
    c_in = f64(c_input)[:, 0, :]
    alpha = sigmoid((xq @ mxq(f64(alpha_weight_ih), 0, "e4m3")) + f64(alpha_bias) + c_in @ f64(alpha_weight_hh))
    e_i = np.exp(i_gate)
    e_a = np.exp(alpha)
    denom = e_i + e_a
    w_i = e_i / denom
    w_a = e_a / denom
    c_1 = w_i * g + w_a * c_in
    h_1 = o_gate * np.tanh(c_1)
    return (h_1, c_1)

@@ -1,0 +1,322 @@
+from contextlib import ExitStack
+
+import concourse.masks as masks
+import concourse.mybir as mybir
+
+BF16 = mybir.dt.bfloat16
+F32 = mybir.dt.float32
+U32 = mybir.dt.uint32
+U8 = mybir.dt.uint8
+FP8X4 = mybir.dt.float8_e4m3fn_x4
+ACT = mybir.ActivationFunctionType
+ALU = mybir.AluOpType
+
+P = 128
+B = 1024
+K_IN = 2048
+H = 256
+PACK = 4
+K_PASS = P * PACK
+PASSES = K_IN // K_PASS
+ROW_TILES = B // P
+IH_COLS = 3 * H
+GATE_COLS = 4 * H
+BANK = 512
+HALVES = GATE_COLS // BANK
+K_TILES_H = H // P
+RUN = 4
+
+X_AHEAD = 3
+Q_AHEAD = 2
+
+FLOPS = 2 * B * K_IN * GATE_COLS + 2 * B * H * GATE_COLS
+
+
+def tile_multiinputlstmcell_pa_kernel(
+    tc,
+    input_,
+    c_input,
+    h_0,
+    weight_ih,
+    weight_hh,
+    alpha_weight_ih,
+    alpha_weight_hh,
+    bias,
+    alpha_bias,
+    out_0,
+    out_1,
+):
+    nc = tc.nc
+    with ExitStack() as ctx:
+        const = ctx.enter_context(tc.tile_pool(name="const", bufs=1))
+        x_pool = ctx.enter_context(tc.tile_pool(name="x_pool", bufs=5))
+        stage = ctx.enter_context(tc.tile_pool(name="stage", bufs=3))
+        work = ctx.enter_context(tc.tile_pool(name="work", bufs=3))
+        psum = ctx.enter_context(tc.psum_pool(name="psum", bufs=8))
+        ctx.enter_context(tc.manual_schedule())
+
+        x_view = input_.rearrange("(p m) k -> p m k", m=ROW_TILES)
+        h1_view = out_0.rearrange("(p m) k -> p m k", m=ROW_TILES)
+        c1_view = out_1.rearrange("(p m) k -> p m k", m=ROW_TILES)
+
+        ident_bf = const.tile([P, P], BF16, name="ident_bf")
+        masks.make_identity(nc, ident_bf[:])
+        ident_f32 = const.tile([P, P], F32, name="ident_f32")
+        masks.make_identity(nc, ident_f32[:])
+        ones = const.tile([P, P], BF16, name="ones")
+        nc.vector.memset(ones[:], 1.0)
+        bias_row = const.tile([P, GATE_COLS], BF16, name="bias_row")
+        nc.vector.memset(bias_row[:], 0.0)
+
+        h_rows = const.tile([P, ROW_TILES, H], BF16, name="h_rows")
+        nc.sync.dma_start(out=h_rows[:], in_=h_0.rearrange("(p m) k -> p m k", m=ROW_TILES))
+        c_rows = const.tile([P, ROW_TILES, H], BF16, name="c_rows")
+        nc.sync.dma_start(
+            out=c_rows[:],
+            in_=c_input.flatten_outer_dims().rearrange("(p m) k -> p m k", m=ROW_TILES),
+        )
+        whh = const.tile([P, K_TILES_H, IH_COLS], BF16, name="whh")
+        nc.sync.dma_start(out=whh[:], in_=weight_hh.rearrange("(kt p) n -> p kt n", p=P))
+        awhh = const.tile([P, K_TILES_H, H], BF16, name="awhh")
+        nc.sync.dma_start(out=awhh[:], in_=alpha_weight_hh.rearrange("(kt p) n -> p kt n", p=P))
+        bias_2d = bias.unsqueeze(0)
+        nc.sync.dma_start(out=bias_row[0:1, 0:H], in_=bias_2d[:, 0:H])
+        nc.sync.dma_start(out=bias_row[0:1, H:BANK], in_=alpha_bias.unsqueeze(0))
+        nc.sync.dma_start(out=bias_row[0:1, BANK:GATE_COLS], in_=bias_2d[:, H:IH_COLS])
+
+        raw_ih = []
+        raw_al = []
+        for g in range(PASSES):
+            rows = slice(g * K_PASS, (g + 1) * K_PASS)
+            ih = const.tile([P, PACK * IH_COLS], BF16, name="raw_ih%d" % g)
+            nc.sync.dma_start(
+                out=ih[:].rearrange("p (t c) -> p t c", t=PACK),
+                in_=weight_ih[rows, :].rearrange("(p t) c -> p t c", t=PACK),
+            )
+            al = const.tile([P, PACK * H], BF16, name="raw_al%d" % g)
+            nc.sync.dma_start(
+                out=al[:].rearrange("p (t c) -> p t c", t=PACK),
+                in_=alpha_weight_ih[rows, :].rearrange("(p t) c -> p t c", t=PACK),
+            )
+            raw_ih.append(ih)
+            raw_al.append(al)
+
+        x_rows = {}
+        for m in range(ROW_TILES):
+            x_rows[m] = x_pool.tile([P, K_IN], BF16, name="x_rows")
+            nc.sync.dma_start(out=x_rows[m][:], in_=x_view[:, m, :])
+
+        hc_t = const.tile([P, ROW_TILES, 2 * K_TILES_H, P], BF16, name="hc_t")
+        h1_all = const.tile([P, ROW_TILES, H], F32, name="h1_all")
+        c1_all = const.tile([P, ROW_TILES, H], F32, name="c1_all")
+        w_codes = []
+        w_scales = []
+        for g in range(PASSES):
+            w_codes.append(const.tile([P, GATE_COLS], U32, name="w_codes%d" % g, align_bytes=64))
+            w_scales.append(const.tile([P, GATE_COLS], U8, name="w_scales%d" % g, align_bytes=64))
+        x_codes = []
+        x_scales = []
+        plain = []
+        for m in range(ROW_TILES):
+            x_codes.append(const.tile([P, PASSES * P], U32, name="x_codes%d" % m, align_bytes=64))
+            x_scales.append(const.tile([P, PASSES * P], U8, name="x_scales%d" % m, align_bytes=64))
+            plain.append(const.tile([P, GATE_COLS], F32, name="plain%d" % m))
+
+        hc_bank = {}
+        plain_bank = {}
+        grouped_w = {}
+        x_bank = {}
+        grouped_x = {}
+        mx_bank = {}
+        gates = {}
+        w_i = {}
+        mix = {}
+        tanh_c1 = {}
+
+        def transpose_hc(m):
+            hc_bank[m] = psum.tile([P, 2 * K_TILES_H, P], BF16, name="hc_bank", tag="bank")
+            for kt in range(K_TILES_H):
+                cols = slice(kt * P, (kt + 1) * P)
+                nc.tensor.transpose(hc_bank[m][:, kt, :], h_rows[:, m, cols], ident_bf[:])
+                nc.tensor.transpose(hc_bank[m][:, K_TILES_H + kt, :], c_rows[:, m, cols], ident_bf[:])
+
+        def copy_hc(m):
+            nc.scalar.copy(out=hc_t[:, m, :, :], in_=hc_bank[m][:])
+
+        def plain_matmuls(m):
+            ia = psum.tile([P, BANK], F32, name="ia", tag="bank")
+            og = psum.tile([P, BANK], F32, name="og", tag="bank")
+            plain_bank[m] = [ia, og]
+            last = K_TILES_H - 1
+            nc.tensor.matmul(ia[:, 0:H], lhsT=ones[:], rhs=bias_row[:, 0:H], start=True, stop=False)
+            for kt in range(K_TILES_H):
+                nc.tensor.matmul(
+                    ia[:, 0:H], lhsT=hc_t[:, m, kt, :], rhs=whh[:, kt, 0:H], start=False, stop=(kt == last)
+                )
+            nc.tensor.matmul(ia[:, H:BANK], lhsT=ones[:], rhs=bias_row[:, H:BANK], start=True, stop=False)
+            for kt in range(K_TILES_H):
+                nc.tensor.matmul(
+                    ia[:, H:BANK],
+                    lhsT=hc_t[:, m, K_TILES_H + kt, :],
+                    rhs=awhh[:, kt, :],
+                    start=False,
+                    stop=(kt == last),
+                )
+            nc.tensor.matmul(og[:], lhsT=ones[:], rhs=bias_row[:, BANK:GATE_COLS], start=True, stop=False)
+            for kt in range(K_TILES_H):
+                nc.tensor.matmul(
+                    og[:], lhsT=hc_t[:, m, kt, :], rhs=whh[:, kt, H:IH_COLS], start=False, stop=(kt == last)
+                )
+
+        def copy_plain(m):
+            for n in range(HALVES):
+                nc.scalar.copy(out=plain[m][:, n * BANK : (n + 1) * BANK], in_=plain_bank[m][n][:])
+
+        def regroup_w(g, n):
+            grouped_w[g, n] = stage.tile([P, BANK * PACK], BF16, name="grouped_w", align_bytes=64, bufs=4)
+            dst = grouped_w[g, n][:].rearrange("p (c i t) -> p c t i", i=RUN, t=PACK)
+            ih_src = raw_ih[g][:].rearrange("p (t c i) -> p c t i", t=PACK, i=RUN)
+            al_src = raw_al[g][:].rearrange("p (t c i) -> p c t i", t=PACK, i=RUN)
+            if n == 0:
+                nc.vector.tensor_copy(out=dst[:, 0 : H // RUN], in_=ih_src[:, 0 : H // RUN])
+                nc.vector.tensor_copy(out=dst[:, H // RUN : BANK // RUN], in_=al_src)
+            else:
+                nc.vector.tensor_copy(out=dst, in_=ih_src[:, H // RUN : IH_COLS // RUN])
+
+        def quantise_w(g, n):
+            cols = slice(n * BANK, (n + 1) * BANK)
+            nc.vector.quantize_mx(
+                out=w_codes[g][:, cols].bitcast(FP8X4), scales=w_scales[g][:, cols], in_=grouped_w[g, n][:]
+            )
+
+        def transpose_x(m):
+            x_words = x_rows[m][:].bitcast(F32)
+            x_bank[m] = []
+            for b in range(PASSES // 2):
+                bank = psum.tile([P, 4, P], F32, name="x_bank", tag="bank")
+                for j in range(4):
+                    g, u = 2 * b + j // 2, j % 2
+                    nc.tensor.transpose(
+                        bank[:, j, :], x_words[:, 2 * P * g + u : 2 * P * (g + 1) : 2], ident_f32[:]
+                    )
+                x_bank[m].append(bank)
+
+        def copy_x(m):
+            grouped_x[m] = stage.tile([P, PASSES * P * PACK], BF16, name="grouped_x", align_bytes=64)
+            words = grouped_x[m][:].bitcast(F32).rearrange("p (g r u) -> p g r u", g=PASSES, u=2)
+            for b in range(PASSES // 2):
+                nc.scalar.copy(
+                    out=words[:, 2 * b : 2 * b + 2, :, :],
+                    in_=x_bank[m][b][:].rearrange("p (g u) r -> p g r u", u=2),
+                )
+
+        def quantise_x(m):
+            nc.vector.quantize_mx(out=x_codes[m][:].bitcast(FP8X4), scales=x_scales[m][:], in_=grouped_x[m][:])
+
+        def mx_matmuls(m):
+            mx_bank[m] = []
+            for n in range(HALVES):
+                cols = slice(n * BANK, (n + 1) * BANK)
+                bank = psum.tile([P, BANK], F32, name="mx_bank", tag="bank")
+                for g in range(PASSES):
+                    nc.tensor.matmul_mx(
+                        out=bank[:],
+                        lhsT=x_codes[m][:, g * P : (g + 1) * P].bitcast(FP8X4),
+                        lhsT_scale=x_scales[m][:, g * P : (g + 1) * P],
+                        rhs=w_codes[g][:, cols].bitcast(FP8X4),
+                        rhs_scale=w_scales[g][:, cols],
+                        start=(g == 0),
+                        stop=(g == PASSES - 1),
+                    )
+                mx_bank[m].append(bank)
+
+        def add_plain(m, n):
+            if n == 0:
+                gates[m] = work.tile([P, GATE_COLS], F32, name="gates")
+            cols = slice(n * BANK, (n + 1) * BANK)
+            nc.vector.tensor_tensor(out=gates[m][:, cols], in0=mx_bank[m][n][:], in1=plain[m][:, cols], op=ALU.add)
+
+        def activate_i_alpha(m):
+            nc.scalar.activation(out=gates[m][:, 0:BANK], in_=gates[m][:, 0:BANK], func=ACT.Sigmoid)
+
+        def activate_o_g(m):
+            nc.scalar.activation(out=gates[m][:, BANK : BANK + H], in_=gates[m][:, BANK : BANK + H], func=ACT.Sigmoid)
+            nc.scalar.activation(out=gates[m][:, BANK + H :], in_=gates[m][:, BANK + H :], func=ACT.Tanh)
+
+        def gate_difference(m):
+            w_i[m] = work.tile([P, H], F32, name="w_i")
+            nc.vector.tensor_tensor(out=w_i[m][:], in0=gates[m][:, 0:H], in1=gates[m][:, H:BANK], op=ALU.subtract)
+
+        def softmax_weight(m):
+            nc.scalar.activation(out=w_i[m][:], in_=w_i[m][:], func=ACT.Sigmoid)
+
+        def cell_difference(m):
+            mix[m] = work.tile([P, H], F32, name="mix")
+            nc.vector.tensor_tensor(out=mix[m][:], in0=gates[m][:, BANK + H :], in1=c_rows[:, m, :], op=ALU.subtract)
+
+        def weigh_difference(m):
+            nc.vector.tensor_tensor(out=mix[m][:], in0=mix[m][:], in1=w_i[m][:], op=ALU.mult)
+
+        def new_cell(m):
+            nc.vector.tensor_tensor(out=c1_all[:, m, :], in0=mix[m][:], in1=c_rows[:, m, :], op=ALU.add)
+
+        def tanh_cell(m):
+            tanh_c1[m] = work.tile([P, H], F32, name="tanh_c1")
+            nc.scalar.activation(out=tanh_c1[m][:], in_=c1_all[:, m, :], func=ACT.Tanh)
+
+        def new_hidden(m):
+            nc.vector.tensor_tensor(out=h1_all[:, m, :], in0=gates[m][:, BANK : BANK + H], in1=tanh_c1[m][:], op=ALU.mult)
+
+        def store_pair(view, rows, m):
+            pair = slice(m - 1, m + 1)
+            nc.sync.dma_start(out=view[:, pair, :], in_=rows[:, pair, :])
+
+        for m in range(ROW_TILES + 1):
+            if m < ROW_TILES:
+                transpose_hc(m)
+            if m >= 1:
+                copy_hc(m - 1)
+        plain_matmuls(0)
+        for g in range(PASSES):
+            regroup_w(g, 0)
+            regroup_w(g, 1)
+            for n in range(HALVES):
+                m = HALVES * g + n
+                if m + 1 < ROW_TILES:
+                    plain_matmuls(m + 1)
+                copy_plain(m)
+                quantise_w(g, n)
+
+        for step in range(-X_AHEAD, ROW_TILES + 1):
+            m = step
+            now = 0 <= m < ROW_TILES
+            before = 1 <= m
+            if now:
+                mx_matmuls(m)
+            if m + X_AHEAD < ROW_TILES:
+                transpose_x(m + X_AHEAD)
+            if now:
+                add_plain(m, 0)
+                activate_i_alpha(m)
+            if before:
+                weigh_difference(m - 1)
+            if now:
+                add_plain(m, 1)
+                activate_o_g(m)
+            if before:
+                new_cell(m - 1)
+                tanh_cell(m - 1)
+                if (m - 1) % 2 == 1:
+                    store_pair(c1_view, c1_all, m - 1)
+            if 0 <= m + Q_AHEAD < ROW_TILES:
+                quantise_x(m + Q_AHEAD)
+            if now:
+                gate_difference(m)
+                softmax_weight(m)
+                cell_difference(m)
+            if m + X_AHEAD < ROW_TILES:
+                copy_x(m + X_AHEAD)
+            if before:
+                new_hidden(m - 1)
+                if (m - 1) % 2 == 1:
+                    store_pair(h1_view, h1_all, m - 1)

@@ -49,7 +49,7 @@ def tile_multiinputlstmcell_pa_kernel(
     nc = tc.nc
     with ExitStack() as ctx:
         const = ctx.enter_context(tc.tile_pool(name="const", bufs=1))
-        x_pool = ctx.enter_context(tc.tile_pool(name="x_pool", bufs=5))
+        x_pool = ctx.enter_context(tc.tile_pool(name="x_pool", bufs=6))
         stage = ctx.enter_context(tc.tile_pool(name="stage", bufs=3))
         work = ctx.enter_context(tc.tile_pool(name="work", bufs=3))
         psum = ctx.enter_context(tc.psum_pool(name="psum", bufs=8))
@@ -59,8 +59,6 @@ def tile_multiinputlstmcell_pa_kernel(
         h1_view = out_0.rearrange("(p m) k -> p m k", m=ROW_TILES)
         c1_view = out_1.rearrange("(p m) k -> p m k", m=ROW_TILES)
 
-        ident_bf = const.tile([P, P], BF16, name="ident_bf")
-        masks.make_identity(nc, ident_bf[:])
         ident_f32 = const.tile([P, P], F32, name="ident_f32")
         masks.make_identity(nc, ident_f32[:])
         ones = const.tile([P, P], BF16, name="ones")
@@ -69,44 +67,89 @@ def tile_multiinputlstmcell_pa_kernel(
         nc.vector.memset(bias_row[:], 0.0)
 
         h_rows = const.tile([P, ROW_TILES, H], BF16, name="h_rows")
-        nc.sync.dma_start(out=h_rows[:], in_=h_0.rearrange("(p m) k -> p m k", m=ROW_TILES))
         c_rows = const.tile([P, ROW_TILES, H], BF16, name="c_rows")
-        nc.sync.dma_start(
-            out=c_rows[:],
-            in_=c_input.flatten_outer_dims().rearrange("(p m) k -> p m k", m=ROW_TILES),
-        )
         whh = const.tile([P, K_TILES_H, IH_COLS], BF16, name="whh")
-        nc.sync.dma_start(out=whh[:], in_=weight_hh.rearrange("(kt p) n -> p kt n", p=P))
         awhh = const.tile([P, K_TILES_H, H], BF16, name="awhh")
-        nc.sync.dma_start(out=awhh[:], in_=alpha_weight_hh.rearrange("(kt p) n -> p kt n", p=P))
-        bias_2d = bias.unsqueeze(0)
-        nc.sync.dma_start(out=bias_row[0:1, 0:H], in_=bias_2d[:, 0:H])
-        nc.sync.dma_start(out=bias_row[0:1, H:BANK], in_=alpha_bias.unsqueeze(0))
-        nc.sync.dma_start(out=bias_row[0:1, BANK:GATE_COLS], in_=bias_2d[:, H:IH_COLS])
-
         raw_ih = []
         raw_al = []
         for g in range(PASSES):
-            rows = slice(g * K_PASS, (g + 1) * K_PASS)
-            ih = const.tile([P, PACK * IH_COLS], BF16, name="raw_ih%d" % g)
+            raw_ih.append(const.tile([P, PACK * IH_COLS], BF16, name="raw_ih%d" % g))
+            raw_al.append(const.tile([P, PACK * H], BF16, name="raw_al%d" % g))
+
+        def load_ih(g):
             nc.sync.dma_start(
-                out=ih[:].rearrange("p (t c) -> p t c", t=PACK),
-                in_=weight_ih[rows, :].rearrange("(p t) c -> p t c", t=PACK),
+                out=raw_ih[g][:].rearrange("p (t c) -> p t c", t=PACK),
+                in_=weight_ih[g * K_PASS : (g + 1) * K_PASS, :].rearrange("(p t) c -> p t c", t=PACK),
             )
-            al = const.tile([P, PACK * H], BF16, name="raw_al%d" % g)
+
+        def load_al(g):
             nc.sync.dma_start(
-                out=al[:].rearrange("p (t c) -> p t c", t=PACK),
-                in_=alpha_weight_ih[rows, :].rearrange("(p t) c -> p t c", t=PACK),
+                out=raw_al[g][:].rearrange("p (t c) -> p t c", t=PACK),
+                in_=alpha_weight_ih[g * K_PASS : (g + 1) * K_PASS, :].rearrange("(p t) c -> p t c", t=PACK),
             )
-            raw_ih.append(ih)
-            raw_al.append(al)
+
+        h_view = h_0.rearrange("(p m) k -> p m k", m=ROW_TILES)
+        c_view = c_input.flatten_outer_dims().rearrange("(p m) k -> p m k", m=ROW_TILES)
+        half = ROW_TILES // 2
+        def load_h(part):
+            nc.sync.dma_start(out=h_rows[:, part, :], in_=h_view[:, part, :])
+
+        def load_c(part):
+            nc.sync.dma_start(out=c_rows[:, part, :], in_=c_view[:, part, :])
+
+        def load_whh(cols):
+            nc.sync.dma_start(out=whh[:, :, cols], in_=weight_hh.rearrange("(p e) n -> p e n", e=2)[:, :, cols])
+
+        def load_awhh():
+            nc.sync.dma_start(out=awhh[:], in_=alpha_weight_hh.rearrange("(p e) n -> p e n", e=2))
+
+        def load_ih_part(g, cols):
+            nc.sync.dma_start(
+                out=raw_ih[g][:].rearrange("p (t c) -> p t c", t=PACK)[:, :, cols],
+                in_=weight_ih[g * K_PASS : (g + 1) * K_PASS, cols].rearrange("(p t) c -> p t c", t=PACK),
+            )
+
+        def load_bias():
+            nc.sync.dma_start(out=bias_row[0:1, H:GATE_COLS], in_=bias.unsqueeze(0))
+
+        def load_alpha_bias():
+            nc.sync.dma_start(out=bias_row[0:1, 0:H], in_=alpha_bias.unsqueeze(0))
 
         x_rows = {}
-        for m in range(ROW_TILES):
+
+        def load_x(m):
             x_rows[m] = x_pool.tile([P, K_IN], BF16, name="x_rows")
             nc.sync.dma_start(out=x_rows[m][:], in_=x_view[:, m, :])
 
-        hc_t = const.tile([P, ROW_TILES, 2 * K_TILES_H, P], BF16, name="hc_t")
+        first, second = slice(0, half), slice(half, ROW_TILES)
+        i_cols, og_cols = slice(0, H), slice(H, IH_COLS)
+        load_h(first)
+        load_whh(og_cols)
+        load_bias()
+        load_al(0)
+        load_ih_part(0, i_cols)
+        load_ih_part(0, og_cols)
+        load_whh(i_cols)
+        load_c(first)
+        load_awhh()
+        load_alpha_bias()
+        load_al(1)
+        load_ih(1)
+        load_h(second)
+        load_c(second)
+        load_al(2)
+        load_ih(2)
+        load_al(3)
+        load_ih(3)
+        load_x(0)
+        load_x(1)
+        load_x(2)
+        load_x(3)
+        load_x(4)
+        load_x(5)
+        load_x(6)
+        load_x(7)
+        hc_t = const.tile([P, ROW_TILES, 2, P], F32, name="hc_t")
         h1_all = const.tile([P, ROW_TILES, H], F32, name="h1_all")
         c1_all = const.tile([P, ROW_TILES, H], F32, name="c1_all")
         w_codes = []
@@ -133,61 +176,58 @@ def tile_multiinputlstmcell_pa_kernel(
         mix = {}
         tanh_c1 = {}
 
-        def transpose_hc(m):
-            hc_bank[m] = psum.tile([P, 2 * K_TILES_H, P], BF16, name="hc_bank", tag="bank")
-            for kt in range(K_TILES_H):
-                cols = slice(kt * P, (kt + 1) * P)
-                nc.tensor.transpose(hc_bank[m][:, kt, :], h_rows[:, m, cols], ident_bf[:])
-                nc.tensor.transpose(hc_bank[m][:, K_TILES_H + kt, :], c_rows[:, m, cols], ident_bf[:])
+        def transpose_hidden(m, s, rows):
+            hc_bank[m, s] = psum.tile([P, P], F32, name="hc_bank", tag="bank")
+            nc.tensor.transpose(hc_bank[m, s][:], rows[:, m, :].bitcast(F32), ident_f32[:])
 
-        def copy_hc(m):
-            nc.scalar.copy(out=hc_t[:, m, :, :], in_=hc_bank[m][:])
+        def copy_hidden(m, s):
+            nc.scalar.copy(out=hc_t[:, m, s, :], in_=hc_bank[m, s][:])
 
-        def plain_matmuls(m):
-            ia = psum.tile([P, BANK], F32, name="ia", tag="bank")
-            og = psum.tile([P, BANK], F32, name="og", tag="bank")
-            plain_bank[m] = [ia, og]
-            last = K_TILES_H - 1
-            nc.tensor.matmul(ia[:, 0:H], lhsT=ones[:], rhs=bias_row[:, 0:H], start=True, stop=False)
-            for kt in range(K_TILES_H):
+        def plain_group(out, m, s, weights, bias_cols):
+            for e in range(K_TILES_H):
                 nc.tensor.matmul(
-                    ia[:, 0:H], lhsT=hc_t[:, m, kt, :], rhs=whh[:, kt, 0:H], start=False, stop=(kt == last)
+                    out,
+                    lhsT=hc_t[:, m, s, :].bitcast(BF16)[:, e::2],
+                    rhs=weights[:, e, :],
+                    start=(e == 0),
+                    stop=False,
                 )
-            nc.tensor.matmul(ia[:, H:BANK], lhsT=ones[:], rhs=bias_row[:, H:BANK], start=True, stop=False)
-            for kt in range(K_TILES_H):
-                nc.tensor.matmul(
-                    ia[:, H:BANK],
-                    lhsT=hc_t[:, m, K_TILES_H + kt, :],
-                    rhs=awhh[:, kt, :],
-                    start=False,
-                    stop=(kt == last),
-                )
-            nc.tensor.matmul(og[:], lhsT=ones[:], rhs=bias_row[:, BANK:GATE_COLS], start=True, stop=False)
-            for kt in range(K_TILES_H):
-                nc.tensor.matmul(
-                    og[:], lhsT=hc_t[:, m, kt, :], rhs=whh[:, kt, H:IH_COLS], start=False, stop=(kt == last)
-                )
+            nc.tensor.matmul(out, lhsT=ones[:], rhs=bias_row[:, bias_cols], start=False, stop=True)
 
-        def copy_plain(m):
-            for n in range(HALVES):
-                nc.scalar.copy(out=plain[m][:, n * BANK : (n + 1) * BANK], in_=plain_bank[m][n][:])
+        def plain_og(m):
+            plain_bank[m, 1] = psum.tile([P, BANK], F32, name="og", tag="bank")
+            plain_group(plain_bank[m, 1][:], m, 0, whh[:, :, H:IH_COLS], slice(BANK, GATE_COLS))
 
-        def regroup_w(g, n):
-            grouped_w[g, n] = stage.tile([P, BANK * PACK], BF16, name="grouped_w", align_bytes=64, bufs=4)
-            dst = grouped_w[g, n][:].rearrange("p (c i t) -> p c t i", i=RUN, t=PACK)
-            ih_src = raw_ih[g][:].rearrange("p (t c i) -> p c t i", t=PACK, i=RUN)
-            al_src = raw_al[g][:].rearrange("p (t c i) -> p c t i", t=PACK, i=RUN)
-            if n == 0:
-                nc.vector.tensor_copy(out=dst[:, 0 : H // RUN], in_=ih_src[:, 0 : H // RUN])
-                nc.vector.tensor_copy(out=dst[:, H // RUN : BANK // RUN], in_=al_src)
-            else:
-                nc.vector.tensor_copy(out=dst, in_=ih_src[:, H // RUN : IH_COLS // RUN])
+        def plain_ai(m):
+            plain_bank[m, 0] = psum.tile([P, BANK], F32, name="ai", tag="bank")
+            plain_group(plain_bank[m, 0][:, H:BANK], m, 0, whh[:, :, 0:H], slice(H, BANK))
+            plain_group(plain_bank[m, 0][:, 0:H], m, 1, awhh, slice(0, H))
 
-        def quantise_w(g, n):
-            cols = slice(n * BANK, (n + 1) * BANK)
-            nc.vector.quantize_mx(
-                out=w_codes[g][:, cols].bitcast(FP8X4), scales=w_scales[g][:, cols], in_=grouped_w[g, n][:]
+        def copy_plain(m, n):
+            nc.scalar.copy(out=plain[m][:, n * BANK : (n + 1) * BANK], in_=plain_bank[m, n][:])
+
+        def regroup(dst, src):
+            nc.vector.tensor_copy(
+                out=dst.rearrange("p (c i t) -> p c t i", i=RUN, t=PACK),
+                in_=src.rearrange("p (t c i) -> p c t i", t=PACK, i=RUN),
             )
+
+        def regroup_al(g):
+            grouped_w[g] = stage.tile([P, GATE_COLS * PACK], BF16, name="grouped_w", align_bytes=64, bufs=2)
+            regroup(grouped_w[g][:, 0 : H * PACK], raw_al[g][:])
+
+        def regroup_ih(g):
+            regroup(grouped_w[g][:, H * PACK :], raw_ih[g][:])
+
+        def regroup_ih_part(g, cols):
+            dst = grouped_w[g][:, (H + cols.start) * PACK : (H + cols.stop) * PACK]
+            nc.vector.tensor_copy(
+                out=dst.rearrange("p (c i t) -> p c t i", i=RUN, t=PACK),
+                in_=raw_ih[g][:].rearrange("p (t c) -> p t c", t=PACK)[:, :, cols].rearrange("p t (c i) -> p c t i", i=RUN),
+            )
+
+        def quantise_w(g):
+            nc.vector.quantize_mx(out=w_codes[g][:].bitcast(FP8X4), scales=w_scales[g][:], in_=grouped_w[g][:])
 
         def transpose_x(m):
             x_words = x_rows[m][:].bitcast(F32)
@@ -201,8 +241,11 @@ def tile_multiinputlstmcell_pa_kernel(
                     )
                 x_bank[m].append(bank)
 
-        def copy_x(m):
+        def open_x(m):
             grouped_x[m] = stage.tile([P, PASSES * P * PACK], BF16, name="grouped_x", align_bytes=64)
+
+        def copy_x(m):
+            open_x(m)
             words = grouped_x[m][:].bitcast(F32).rearrange("p (g r u) -> p g r u", g=PASSES, u=2)
             for b in range(PASSES // 2):
                 nc.scalar.copy(
@@ -213,14 +256,10 @@ def tile_multiinputlstmcell_pa_kernel(
         def quantise_x(m):
             nc.vector.quantize_mx(out=x_codes[m][:].bitcast(FP8X4), scales=x_scales[m][:], in_=grouped_x[m][:])
 
-        def mx_matmuls(m):
-            mx_bank[m] = []
-            for n in range(HALVES):
-                cols = slice(n * BANK, (n + 1) * BANK)
-                bank = psum.tile([P, BANK], F32, name="mx_bank", tag="bank")
+        def mx_group(m, out, cols):
                 for g in range(PASSES):
                     nc.tensor.matmul_mx(
-                        out=bank[:],
+                        out=out,
                         lhsT=x_codes[m][:, g * P : (g + 1) * P].bitcast(FP8X4),
                         lhsT_scale=x_scales[m][:, g * P : (g + 1) * P],
                         rhs=w_codes[g][:, cols].bitcast(FP8X4),
@@ -228,24 +267,30 @@ def tile_multiinputlstmcell_pa_kernel(
                         start=(g == 0),
                         stop=(g == PASSES - 1),
                     )
-                mx_bank[m].append(bank)
 
-        def add_plain(m, n):
+        def mx_matmuls(m):
+            mx_bank[m] = [psum.tile([P, BANK], F32, name="mx_bank%d" % n, tag="bank") for n in range(HALVES)]
+            mx_group(m, mx_bank[m][0][:], slice(0, BANK))
+            mx_group(m, mx_bank[m][1][:], slice(BANK, GATE_COLS))
+
+        def add_plain(m, n, part=slice(0, BANK)):
             if n == 0:
                 gates[m] = work.tile([P, GATE_COLS], F32, name="gates")
-            cols = slice(n * BANK, (n + 1) * BANK)
-            nc.vector.tensor_tensor(out=gates[m][:, cols], in0=mx_bank[m][n][:], in1=plain[m][:, cols], op=ALU.add)
+            cols = slice(n * BANK + part.start, n * BANK + part.stop)
+            nc.vector.tensor_tensor(out=gates[m][:, cols], in0=mx_bank[m][n][:, part], in1=plain[m][:, cols], op=ALU.add)
 
         def activate_i_alpha(m):
             nc.scalar.activation(out=gates[m][:, 0:BANK], in_=gates[m][:, 0:BANK], func=ACT.Sigmoid)
 
-        def activate_o_g(m):
+        def activate_o(m):
             nc.scalar.activation(out=gates[m][:, BANK : BANK + H], in_=gates[m][:, BANK : BANK + H], func=ACT.Sigmoid)
+
+        def activate_g(m):
             nc.scalar.activation(out=gates[m][:, BANK + H :], in_=gates[m][:, BANK + H :], func=ACT.Tanh)
 
         def gate_difference(m):
             w_i[m] = work.tile([P, H], F32, name="w_i")
-            nc.vector.tensor_tensor(out=w_i[m][:], in0=gates[m][:, 0:H], in1=gates[m][:, H:BANK], op=ALU.subtract)
+            nc.vector.tensor_tensor(out=w_i[m][:], in0=gates[m][:, H:BANK], in1=gates[m][:, 0:H], op=ALU.subtract)
 
         def softmax_weight(m):
             nc.scalar.activation(out=w_i[m][:], in_=w_i[m][:], func=ACT.Sigmoid)
@@ -271,30 +316,69 @@ def tile_multiinputlstmcell_pa_kernel(
             pair = slice(m - 1, m + 1)
             nc.sync.dma_start(out=view[:, pair, :], in_=rows[:, pair, :])
 
-        for m in range(ROW_TILES + 1):
-            if m < ROW_TILES:
-                transpose_hc(m)
-            if m >= 1:
-                copy_hc(m - 1)
-        plain_matmuls(0)
-        for g in range(PASSES):
-            regroup_w(g, 0)
-            regroup_w(g, 1)
-            for n in range(HALVES):
-                m = HALVES * g + n
-                if m + 1 < ROW_TILES:
-                    plain_matmuls(m + 1)
-                copy_plain(m)
-                quantise_w(g, n)
+        for m in range(half):
+            transpose_hidden(m, 0, h_rows)
+            copy_hidden(m, 0)
+        regroup_al(0)
+        regroup_ih_part(0, i_cols)
+        regroup_ih_part(0, og_cols)
+        for m in range(half):
+            plain_og(m)
+            copy_plain(m, 1)
+        for m in range(half):
+            transpose_hidden(m, 1, c_rows)
+            copy_hidden(m, 1)
+        regroup_al(1)
+        quantise_w(0)
+        regroup_ih(1)
+        for m in range(half):
+            plain_ai(m)
+            copy_plain(m, 0)
+        regroup_al(2)
+        quantise_w(1)
+        regroup_ih(2)
+        for m in range(half, ROW_TILES):
+            transpose_hidden(m, 0, h_rows)
+            copy_hidden(m, 0)
+        for m in range(half, ROW_TILES):
+            transpose_hidden(m, 1, c_rows)
+            copy_hidden(m, 1)
+        plain_og(4)
+        copy_plain(4, 1)
+        plain_ai(4)
+        copy_plain(4, 0)
+        plain_og(5)
+        copy_plain(5, 1)
+        plain_ai(5)
+        copy_plain(5, 0)
+        plain_og(6)
+        copy_plain(6, 1)
+        plain_ai(6)
+        copy_plain(6, 0)
+        transpose_x(0)
+        copy_x(0)
+        plain_og(7)
+        copy_plain(7, 1)
+        plain_ai(7)
+        copy_plain(7, 0)
+        transpose_x(1)
+        copy_x(1)
+        transpose_x(2)
+        copy_x(2)
+        regroup_al(3)
+        quantise_w(2)
+        regroup_ih(3)
+        quantise_x(0)
+        quantise_w(3)
+        quantise_x(1)
 
-        for step in range(-X_AHEAD, ROW_TILES + 1):
-            m = step
-            now = 0 <= m < ROW_TILES
+        for m in range(ROW_TILES + 1):
+            now = m < ROW_TILES
             before = 1 <= m
             if now:
                 mx_matmuls(m)
-            if m + X_AHEAD < ROW_TILES:
-                transpose_x(m + X_AHEAD)
+            if m + 3 < ROW_TILES:
+                transpose_x(m + 3)
             if now:
                 add_plain(m, 0)
                 activate_i_alpha(m)
@@ -302,20 +386,21 @@ def tile_multiinputlstmcell_pa_kernel(
                 weigh_difference(m - 1)
             if now:
                 add_plain(m, 1)
-                activate_o_g(m)
+                activate_o(m)
+                activate_g(m)
             if before:
                 new_cell(m - 1)
                 tanh_cell(m - 1)
                 if (m - 1) % 2 == 1:
                     store_pair(c1_view, c1_all, m - 1)
-            if 0 <= m + Q_AHEAD < ROW_TILES:
-                quantise_x(m + Q_AHEAD)
+            if m + 2 < ROW_TILES:
+                quantise_x(m + 2)
             if now:
                 gate_difference(m)
                 softmax_weight(m)
                 cell_difference(m)
-            if m + X_AHEAD < ROW_TILES:
-                copy_x(m + X_AHEAD)
+            if m + 3 < ROW_TILES:
+                copy_x(m + 3)
             if before:
                 new_hidden(m - 1)
                 if (m - 1) % 2 == 1:

@@ -226,8 +226,12 @@ def tile_multiinputlstmcell_pa_kernel(
                 in_=raw_ih[g][:].rearrange("p (t c) -> p t c", t=PACK)[:, :, cols].rearrange("p t (c i) -> p c t i", i=RUN),
             )
 
-        def quantise_w(g):
-            nc.vector.quantize_mx(out=w_codes[g][:].bitcast(FP8X4), scales=w_scales[g][:], in_=grouped_w[g][:])
+        def quantise_w(g, cols=slice(0, GATE_COLS)):
+            nc.vector.quantize_mx(
+                out=w_codes[g][:, cols].bitcast(FP8X4),
+                scales=w_scales[g][:, cols],
+                in_=grouped_w[g][:, cols.start * PACK : cols.stop * PACK],
+            )
 
         def transpose_x(m):
             x_words = x_rows[m][:].bitcast(F32)
@@ -271,50 +275,62 @@ def tile_multiinputlstmcell_pa_kernel(
         def mx_matmuls(m):
             mx_bank[m] = [psum.tile([P, BANK], F32, name="mx_bank%d" % n, tag="bank") for n in range(HALVES)]
             mx_group(m, mx_bank[m][0][:], slice(0, BANK))
-            mx_group(m, mx_bank[m][1][:], slice(BANK, GATE_COLS))
+            if m < ROW_TILES - 1:
+                mx_group(m, mx_bank[m][1][:], slice(BANK, GATE_COLS))
+            else:
+                mx_group(m, mx_bank[m][1][:, H:BANK], slice(BANK + H, GATE_COLS))
+                mx_group(m, mx_bank[m][1][:, 0:H], slice(BANK, BANK + H))
 
         def add_plain(m, n, part=slice(0, BANK)):
             if n == 0:
                 gates[m] = work.tile([P, GATE_COLS], F32, name="gates")
+                w_i[m] = work.tile([P, H], F32, name="w_i")
+                mix[m] = work.tile([P, H], F32, name="mix")
+                tanh_c1[m] = work.tile([P, H], F32, name="tanh_c1")
             cols = slice(n * BANK + part.start, n * BANK + part.stop)
             nc.vector.tensor_tensor(out=gates[m][:, cols], in0=mx_bank[m][n][:, part], in1=plain[m][:, cols], op=ALU.add)
 
-        def activate_i_alpha(m):
-            nc.scalar.activation(out=gates[m][:, 0:BANK], in_=gates[m][:, 0:BANK], func=ACT.Sigmoid)
+        def activate(m, func, cols):
+            nc.scalar.activation(out=gates[m][:, cols], in_=gates[m][:, cols], func=func)
+
+        def activate_alpha_i(m):
+            activate(m, ACT.Sigmoid, slice(0, BANK))
 
         def activate_o(m):
-            nc.scalar.activation(out=gates[m][:, BANK : BANK + H], in_=gates[m][:, BANK : BANK + H], func=ACT.Sigmoid)
+            activate(m, ACT.Sigmoid, slice(BANK, BANK + H))
 
         def activate_g(m):
-            nc.scalar.activation(out=gates[m][:, BANK + H :], in_=gates[m][:, BANK + H :], func=ACT.Tanh)
+            activate(m, ACT.Tanh, slice(BANK + H, GATE_COLS))
 
-        def gate_difference(m):
-            w_i[m] = work.tile([P, H], F32, name="w_i")
-            nc.vector.tensor_tensor(out=w_i[m][:], in0=gates[m][:, H:BANK], in1=gates[m][:, 0:H], op=ALU.subtract)
+        def gate_difference(m, lo=0, hi=H):
+            nc.vector.tensor_tensor(
+                out=w_i[m][:, lo:hi], in0=gates[m][:, H + lo : H + hi], in1=gates[m][:, lo:hi], op=ALU.subtract
+            )
 
-        def softmax_weight(m):
-            nc.scalar.activation(out=w_i[m][:], in_=w_i[m][:], func=ACT.Sigmoid)
+        def softmax_weight(m, lo=0, hi=H):
+            nc.scalar.activation(out=w_i[m][:, lo:hi], in_=w_i[m][:, lo:hi], func=ACT.Sigmoid)
 
         def cell_difference(m):
-            mix[m] = work.tile([P, H], F32, name="mix")
             nc.vector.tensor_tensor(out=mix[m][:], in0=gates[m][:, BANK + H :], in1=c_rows[:, m, :], op=ALU.subtract)
 
-        def weigh_difference(m):
-            nc.vector.tensor_tensor(out=mix[m][:], in0=mix[m][:], in1=w_i[m][:], op=ALU.mult)
+        def weigh_difference(m, lo=0, hi=H):
+            nc.vector.tensor_tensor(out=mix[m][:, lo:hi], in0=mix[m][:, lo:hi], in1=w_i[m][:, lo:hi], op=ALU.mult)
 
-        def new_cell(m):
-            nc.vector.tensor_tensor(out=c1_all[:, m, :], in0=mix[m][:], in1=c_rows[:, m, :], op=ALU.add)
+        def new_cell(m, lo=0, hi=H):
+            nc.vector.tensor_tensor(
+                out=c1_all[:, m, lo:hi], in0=mix[m][:, lo:hi], in1=c_rows[:, m, lo:hi], op=ALU.add
+            )
 
-        def tanh_cell(m):
-            tanh_c1[m] = work.tile([P, H], F32, name="tanh_c1")
-            nc.scalar.activation(out=tanh_c1[m][:], in_=c1_all[:, m, :], func=ACT.Tanh)
+        def tanh_cell(m, lo=0, hi=H):
+            nc.scalar.activation(out=tanh_c1[m][:, lo:hi], in_=c1_all[:, m, lo:hi], func=ACT.Tanh)
 
-        def new_hidden(m):
-            nc.vector.tensor_tensor(out=h1_all[:, m, :], in0=gates[m][:, BANK : BANK + H], in1=tanh_c1[m][:], op=ALU.mult)
+        def new_hidden(m, lo=0, hi=H):
+            nc.vector.tensor_tensor(
+                out=h1_all[:, m, lo:hi], in0=gates[m][:, BANK + lo : BANK + hi], in1=tanh_c1[m][:, lo:hi], op=ALU.mult
+            )
 
-        def store_pair(view, rows, m):
-            pair = slice(m - 1, m + 1)
-            nc.sync.dma_start(out=view[:, pair, :], in_=rows[:, pair, :])
+        def store(view, rows, first, count):
+            nc.sync.dma_start(out=view[:, first : first + count, :], in_=rows[:, first : first + count, :])
 
         for m in range(half):
             transpose_hidden(m, 0, h_rows)
@@ -368,40 +384,65 @@ def tile_multiinputlstmcell_pa_kernel(
         regroup_al(3)
         quantise_w(2)
         regroup_ih(3)
-        quantise_x(0)
         quantise_w(3)
+        quantise_x(0)
         quantise_x(1)
 
-        for m in range(ROW_TILES + 1):
-            now = m < ROW_TILES
-            before = 1 <= m
-            if now:
-                mx_matmuls(m)
+
+        last = ROW_TILES - 1
+        for m in range(last):
+            mx_matmuls(m)
             if m + 3 < ROW_TILES:
                 transpose_x(m + 3)
-            if now:
-                add_plain(m, 0)
-                activate_i_alpha(m)
-            if before:
+            if m == last - 1:
+                mx_matmuls(last)
+            add_plain(m, 0)
+            activate_alpha_i(m)
+            if m > 0:
                 weigh_difference(m - 1)
-            if now:
-                add_plain(m, 1)
-                activate_o(m)
-                activate_g(m)
-            if before:
+            add_plain(m, 1)
+            activate_o(m)
+            activate_g(m)
+            if m > 0:
                 new_cell(m - 1)
                 tanh_cell(m - 1)
-                if (m - 1) % 2 == 1:
-                    store_pair(c1_view, c1_all, m - 1)
+                if m % 2 == 0:
+                    store(c1_view, c1_all, m - 2, 2)
             if m + 2 < ROW_TILES:
                 quantise_x(m + 2)
-            if now:
-                gate_difference(m)
-                softmax_weight(m)
-                cell_difference(m)
+            gate_difference(m)
+            softmax_weight(m)
+            cell_difference(m)
             if m + 3 < ROW_TILES:
                 copy_x(m + 3)
-            if before:
+            if m > 0:
                 new_hidden(m - 1)
-                if (m - 1) % 2 == 1:
-                    store_pair(h1_view, h1_all, m - 1)
+                if m % 2 == 0:
+                    store(h1_view, h1_all, m - 2, 2)
+        add_plain(last, 0)
+        activate_alpha_i(last)
+        weigh_difference(last - 1)
+        add_plain(last, 1, slice(H, BANK))
+        activate_g(last)
+        new_cell(last - 1)
+        gate_difference(last, 0, P)
+        softmax_weight(last, 0, P)
+        gate_difference(last, P, H)
+        softmax_weight(last, P, H)
+        cell_difference(last)
+        tanh_cell(last - 1)
+        store(c1_view, c1_all, last - 1, 1)
+        add_plain(last, 1, slice(0, H))
+        weigh_difference(last, 0, P)
+        weigh_difference(last, P, H)
+        activate_o(last)
+        new_cell(last, 0, P)
+        new_cell(last, P, H)
+        tanh_cell(last, 0, P)
+        tanh_cell(last, P, H)
+        store(c1_view, c1_all, last, 1)
+        new_hidden(last - 1)
+        store(h1_view, h1_all, last - 1, 1)
+        new_hidden(last, 0, P)
+        new_hidden(last, P, H)
+        store(h1_view, h1_all, last, 1)

@@ -26,6 +26,8 @@ HALVES = GATE_COLS // BANK
 K_TILES_H = H // P
 RUN = 4
 
+VB = 6
+WARM = (BANK, BANK, 448)
 X_AHEAD = 3
 Q_AHEAD = 2
 
@@ -61,7 +63,7 @@ def tile_multiinputlstmcell_pa_kernel(
 
         ident_f32 = const.tile([P, P], F32, name="ident_f32")
         masks.make_identity(nc, ident_f32[:])
-        ones = const.tile([P, P], BF16, name="ones")
+        ones = const.tile([P, BANK], BF16, name="ones")
         nc.vector.memset(ones[:], 1.0)
         bias_row = const.tile([P, GATE_COLS], BF16, name="bias_row")
         nc.vector.memset(bias_row[:], 0.0)
@@ -165,6 +167,7 @@ def tile_multiinputlstmcell_pa_kernel(
             x_scales.append(const.tile([P, PASSES * P], U8, name="x_scales%d" % m, align_bytes=64))
             plain.append(const.tile([P, GATE_COLS], F32, name="plain%d" % m))
 
+        bias_full = const.tile([P, GATE_COLS], F32, name="bias_full")
         hc_bank = {}
         plain_bank = {}
         grouped_w = {}
@@ -184,15 +187,17 @@ def tile_multiinputlstmcell_pa_kernel(
             nc.scalar.copy(out=hc_t[:, m, s, :], in_=hc_bank[m, s][:])
 
         def plain_group(out, m, s, weights, bias_cols):
+            with_bias = m < VB
             for e in range(K_TILES_H):
                 nc.tensor.matmul(
                     out,
                     lhsT=hc_t[:, m, s, :].bitcast(BF16)[:, e::2],
                     rhs=weights[:, e, :],
                     start=(e == 0),
-                    stop=False,
+                    stop=(e == K_TILES_H - 1 and not with_bias),
                 )
-            nc.tensor.matmul(out, lhsT=ones[:], rhs=bias_row[:, bias_cols], start=False, stop=True)
+            if with_bias:
+                nc.tensor.matmul(out, lhsT=ones[:, 0:P], rhs=bias_row[:, bias_cols], start=False, stop=True)
 
         def plain_og(m):
             plain_bank[m, 1] = psum.tile([P, BANK], F32, name="og", tag="bank")
@@ -203,8 +208,23 @@ def tile_multiinputlstmcell_pa_kernel(
             plain_group(plain_bank[m, 0][:, H:BANK], m, 0, whh[:, :, 0:H], slice(H, BANK))
             plain_group(plain_bank[m, 0][:, 0:H], m, 1, awhh, slice(0, H))
 
+        def warm_up():
+            bank = psum.tile([P, BANK], F32, name="warm_bank", tag="bank")
+            for cols in WARM:
+                nc.tensor.matmul(bank[:, 0:cols], lhsT=ones[:, 0:P], rhs=ones[:, 0:cols], start=True, stop=True)
+
+        def spread_bias(n):
+            cols = slice(n * BANK, (n + 1) * BANK)
+            bank = psum.tile([P, BANK], F32, name="bias_bank", tag="bank")
+            nc.tensor.matmul(bank[:], lhsT=ones[:, 0:P], rhs=bias_row[:, cols], start=True, stop=True)
+            nc.scalar.copy(out=bias_full[:, cols], in_=bank[:])
+
         def copy_plain(m, n):
-            nc.scalar.copy(out=plain[m][:, n * BANK : (n + 1) * BANK], in_=plain_bank[m, n][:])
+            cols = slice(n * BANK, (n + 1) * BANK)
+            if m < VB:
+                nc.scalar.copy(out=plain[m][:, cols], in_=plain_bank[m, n][:])
+            else:
+                nc.vector.tensor_tensor(out=plain[m][:, cols], in0=plain_bank[m, n][:], in1=bias_full[:, cols], op=ALU.add)
 
         def regroup(dst, src):
             nc.vector.tensor_copy(
@@ -332,6 +352,7 @@ def tile_multiinputlstmcell_pa_kernel(
         def store(view, rows, first, count):
             nc.sync.dma_start(out=view[:, first : first + count, :], in_=rows[:, first : first + count, :])
 
+        warm_up()
         for m in range(half):
             transpose_hidden(m, 0, h_rows)
             copy_hidden(m, 0)
@@ -353,6 +374,8 @@ def tile_multiinputlstmcell_pa_kernel(
         regroup_al(2)
         quantise_w(1)
         regroup_ih(2)
+        spread_bias(0)
+        spread_bias(1)
         for m in range(half, ROW_TILES):
             transpose_hidden(m, 0, h_rows)
             copy_hidden(m, 0)
@@ -368,15 +391,11 @@ def tile_multiinputlstmcell_pa_kernel(
         plain_ai(5)
         copy_plain(5, 0)
         plain_og(6)
-        copy_plain(6, 1)
         plain_ai(6)
-        copy_plain(6, 0)
         transpose_x(0)
         copy_x(0)
         plain_og(7)
-        copy_plain(7, 1)
         plain_ai(7)
-        copy_plain(7, 0)
         transpose_x(1)
         copy_x(1)
         transpose_x(2)
@@ -386,7 +405,11 @@ def tile_multiinputlstmcell_pa_kernel(
         regroup_ih(3)
         quantise_w(3)
         quantise_x(0)
+        copy_plain(6, 1)
+        copy_plain(6, 0)
         quantise_x(1)
+        copy_plain(7, 1)
+        copy_plain(7, 0)
 
 
         last = ROW_TILES - 1

@@ -169,6 +169,7 @@ def tile_multiinputlstmcell_pa_kernel(
 
         bias_full = const.tile([P, GATE_COLS], F32, name="bias_full")
         hc_bank = {}
+        both_bank = {}
         plain_bank = {}
         grouped_w = {}
         x_bank = {}
@@ -185,6 +186,14 @@ def tile_multiinputlstmcell_pa_kernel(
 
         def copy_hidden(m, s):
             nc.scalar.copy(out=hc_t[:, m, s, :], in_=hc_bank[m, s][:])
+
+        def transpose_both(m):
+            both_bank[m] = psum.tile([P, 2, P], F32, name="both_bank", tag="bank")
+            nc.tensor.transpose(both_bank[m][:, 0, :], h_rows[:, m, :].bitcast(F32), ident_f32[:])
+            nc.tensor.transpose(both_bank[m][:, 1, :], c_rows[:, m, :].bitcast(F32), ident_f32[:])
+
+        def copy_both(m):
+            nc.scalar.copy(out=hc_t[:, m, :, :], in_=both_bank[m][:])
 
         def plain_group(out, m, s, weights, bias_cols):
             with_bias = m < VB
@@ -359,14 +368,15 @@ def tile_multiinputlstmcell_pa_kernel(
         regroup_al(0)
         regroup_ih_part(0, i_cols)
         regroup_ih_part(0, og_cols)
+        quantise_w(0)
         for m in range(half):
             plain_og(m)
+            if m == half - 1:
+                for j in range(half):
+                    transpose_hidden(j, 1, c_rows)
+                    copy_hidden(j, 1)
             copy_plain(m, 1)
-        for m in range(half):
-            transpose_hidden(m, 1, c_rows)
-            copy_hidden(m, 1)
         regroup_al(1)
-        quantise_w(0)
         regroup_ih(1)
         for m in range(half):
             plain_ai(m)
@@ -377,11 +387,8 @@ def tile_multiinputlstmcell_pa_kernel(
         spread_bias(0)
         spread_bias(1)
         for m in range(half, ROW_TILES):
-            transpose_hidden(m, 0, h_rows)
-            copy_hidden(m, 0)
-        for m in range(half, ROW_TILES):
-            transpose_hidden(m, 1, c_rows)
-            copy_hidden(m, 1)
+            transpose_both(m)
+            copy_both(m)
         plain_og(4)
         copy_plain(4, 1)
         plain_ai(4)
@@ -424,8 +431,8 @@ def tile_multiinputlstmcell_pa_kernel(
             if m > 0:
                 weigh_difference(m - 1)
             add_plain(m, 1)
-            activate_o(m)
             activate_g(m)
+            activate_o(m)
             if m > 0:
                 new_cell(m - 1)
                 tanh_cell(m - 1)
@@ -433,31 +440,34 @@ def tile_multiinputlstmcell_pa_kernel(
                     store(c1_view, c1_all, m - 2, 2)
             if m + 2 < ROW_TILES:
                 quantise_x(m + 2)
+            if m == last - 1:
+                add_plain(last, 0)
+                activate_alpha_i(last)
             gate_difference(m)
             softmax_weight(m)
             cell_difference(m)
             if m + 3 < ROW_TILES:
                 copy_x(m + 3)
-            if m > 0:
+            if m < last - 1 and m > 0:
                 new_hidden(m - 1)
                 if m % 2 == 0:
                     store(h1_view, h1_all, m - 2, 2)
-        add_plain(last, 0)
-        activate_alpha_i(last)
-        weigh_difference(last - 1)
         add_plain(last, 1, slice(H, BANK))
         activate_g(last)
-        new_cell(last - 1)
+        new_hidden(last - 2)
+        store(h1_view, h1_all, last - 3, 2)
         gate_difference(last, 0, P)
         softmax_weight(last, 0, P)
         gate_difference(last, P, H)
         softmax_weight(last, P, H)
+        weigh_difference(last - 1)
         cell_difference(last)
+        new_cell(last - 1)
+        weigh_difference(last, 0, P)
         tanh_cell(last - 1)
+        weigh_difference(last, P, H)
         store(c1_view, c1_all, last - 1, 1)
         add_plain(last, 1, slice(0, H))
-        weigh_difference(last, 0, P)
-        weigh_difference(last, P, H)
         activate_o(last)
         new_cell(last, 0, P)
         new_cell(last, P, H)

from contextlib import ExitStack

import concourse.masks as masks
import concourse.mybir as mybir

BF16 = mybir.dt.bfloat16
F32 = mybir.dt.float32
U32 = mybir.dt.uint32
U8 = mybir.dt.uint8
FP8X4 = mybir.dt.float8_e4m3fn_x4
ACT = mybir.ActivationFunctionType
ALU = mybir.AluOpType

P = 128
B = 1024
K_IN = 2048
H = 256
PACK = 4
K_PASS = P * PACK
PASSES = K_IN // K_PASS
ROW_TILES = B // P
IH_COLS = 3 * H
GATE_COLS = 4 * H
BANK = 512
HALVES = GATE_COLS // BANK
K_TILES_H = H // P
RUN = 4

VB = 6
WARM = (BANK, BANK, 448)
X_AHEAD = 3
Q_AHEAD = 2

FLOPS = 2 * B * K_IN * GATE_COLS + 2 * B * H * GATE_COLS


def tile_multiinputlstmcell_pa_kernel(
    tc,
    input_,
    c_input,
    h_0,
    weight_ih,
    weight_hh,
    alpha_weight_ih,
    alpha_weight_hh,
    bias,
    alpha_bias,
    out_0,
    out_1,
):
    nc = tc.nc
    with ExitStack() as ctx:
        const = ctx.enter_context(tc.tile_pool(name="const", bufs=1))
        x_pool = ctx.enter_context(tc.tile_pool(name="x_pool", bufs=6))
        stage = ctx.enter_context(tc.tile_pool(name="stage", bufs=3))
        work = ctx.enter_context(tc.tile_pool(name="work", bufs=3))
        psum = ctx.enter_context(tc.psum_pool(name="psum", bufs=8))
        ctx.enter_context(tc.manual_schedule())

        x_view = input_.rearrange("(p m) k -> p m k", m=ROW_TILES)
        h1_view = out_0.rearrange("(p m) k -> p m k", m=ROW_TILES)
        c1_view = out_1.rearrange("(p m) k -> p m k", m=ROW_TILES)

        ident_f32 = const.tile([P, P], F32, name="ident_f32")
        masks.make_identity(nc, ident_f32[:])
        ones = const.tile([P, BANK], BF16, name="ones")
        nc.vector.memset(ones[:], 1.0)
        bias_row = const.tile([P, GATE_COLS], BF16, name="bias_row")
        nc.vector.memset(bias_row[:], 0.0)

        h_rows = const.tile([P, ROW_TILES, H], BF16, name="h_rows")
        c_rows = const.tile([P, ROW_TILES, H], BF16, name="c_rows")
        whh = const.tile([P, K_TILES_H, IH_COLS], BF16, name="whh")
        awhh = const.tile([P, K_TILES_H, H], BF16, name="awhh")
        raw_ih = []
        raw_al = []
        for g in range(PASSES):
            raw_ih.append(const.tile([P, PACK * IH_COLS], BF16, name="raw_ih%d" % g))
            raw_al.append(const.tile([P, PACK * H], BF16, name="raw_al%d" % g))

        def load_ih(g):
            nc.sync.dma_start(
                out=raw_ih[g][:].rearrange("p (t c) -> p t c", t=PACK),
                in_=weight_ih[g * K_PASS : (g + 1) * K_PASS, :].rearrange("(p t) c -> p t c", t=PACK),
            )

        def load_al(g):
            nc.sync.dma_start(
                out=raw_al[g][:].rearrange("p (t c) -> p t c", t=PACK),
                in_=alpha_weight_ih[g * K_PASS : (g + 1) * K_PASS, :].rearrange("(p t) c -> p t c", t=PACK),
            )

        h_view = h_0.rearrange("(p m) k -> p m k", m=ROW_TILES)
        c_view = c_input.flatten_outer_dims().rearrange("(p m) k -> p m k", m=ROW_TILES)
        half = ROW_TILES // 2
        def load_h(part):
            nc.sync.dma_start(out=h_rows[:, part, :], in_=h_view[:, part, :])

        def load_c(part):
            nc.sync.dma_start(out=c_rows[:, part, :], in_=c_view[:, part, :])

        def load_whh(cols):
            nc.sync.dma_start(out=whh[:, :, cols], in_=weight_hh.rearrange("(p e) n -> p e n", e=2)[:, :, cols])

        def load_awhh():
            nc.sync.dma_start(out=awhh[:], in_=alpha_weight_hh.rearrange("(p e) n -> p e n", e=2))

        def load_ih_part(g, cols):
            nc.sync.dma_start(
                out=raw_ih[g][:].rearrange("p (t c) -> p t c", t=PACK)[:, :, cols],
                in_=weight_ih[g * K_PASS : (g + 1) * K_PASS, cols].rearrange("(p t) c -> p t c", t=PACK),
            )

        def load_bias():
            nc.sync.dma_start(out=bias_row[0:1, H:GATE_COLS], in_=bias.unsqueeze(0))

        def load_alpha_bias():
            nc.sync.dma_start(out=bias_row[0:1, 0:H], in_=alpha_bias.unsqueeze(0))

        x_rows = {}

        def load_x(m):
            x_rows[m] = x_pool.tile([P, K_IN], BF16, name="x_rows")
            nc.sync.dma_start(out=x_rows[m][:], in_=x_view[:, m, :])

        first, second = slice(0, half), slice(half, ROW_TILES)
        i_cols, og_cols = slice(0, H), slice(H, IH_COLS)
        load_h(first)
        load_whh(og_cols)
        load_bias()
        load_al(0)
        load_ih_part(0, i_cols)
        load_ih_part(0, og_cols)
        load_whh(i_cols)
        load_c(first)
        load_awhh()
        load_alpha_bias()
        load_al(1)
        load_ih(1)
        load_h(second)
        load_c(second)
        load_al(2)
        load_ih(2)
        load_al(3)
        load_ih(3)
        load_x(0)
        load_x(1)
        load_x(2)
        load_x(3)
        load_x(4)
        load_x(5)
        load_x(6)
        load_x(7)
        hc_t = const.tile([P, ROW_TILES, 2, P], F32, name="hc_t")
        h1_all = const.tile([P, ROW_TILES, H], F32, name="h1_all")
        c1_all = const.tile([P, ROW_TILES, H], F32, name="c1_all")
        w_codes = []
        w_scales = []
        for g in range(PASSES):
            w_codes.append(const.tile([P, GATE_COLS], U32, name="w_codes%d" % g, align_bytes=64))
            w_scales.append(const.tile([P, GATE_COLS], U8, name="w_scales%d" % g, align_bytes=64))
        x_codes = []
        x_scales = []
        plain = []
        for m in range(ROW_TILES):
            x_codes.append(const.tile([P, PASSES * P], U32, name="x_codes%d" % m, align_bytes=64))
            x_scales.append(const.tile([P, PASSES * P], U8, name="x_scales%d" % m, align_bytes=64))
            plain.append(const.tile([P, GATE_COLS], F32, name="plain%d" % m))

        bias_full = const.tile([P, GATE_COLS], F32, name="bias_full")
        hc_bank = {}
        both_bank = {}
        plain_bank = {}
        grouped_w = {}
        x_bank = {}
        grouped_x = {}
        mx_bank = {}
        gates = {}
        w_i = {}
        mix = {}
        tanh_c1 = {}

        def transpose_hidden(m, s, rows):
            hc_bank[m, s] = psum.tile([P, P], F32, name="hc_bank", tag="bank")
            nc.tensor.transpose(hc_bank[m, s][:], rows[:, m, :].bitcast(F32), ident_f32[:])

        def copy_hidden(m, s):
            nc.scalar.copy(out=hc_t[:, m, s, :], in_=hc_bank[m, s][:])

        def transpose_both(m):
            both_bank[m] = psum.tile([P, 2, P], F32, name="both_bank", tag="bank")
            nc.tensor.transpose(both_bank[m][:, 0, :], h_rows[:, m, :].bitcast(F32), ident_f32[:])
            nc.tensor.transpose(both_bank[m][:, 1, :], c_rows[:, m, :].bitcast(F32), ident_f32[:])

        def copy_both(m):
            nc.scalar.copy(out=hc_t[:, m, :, :], in_=both_bank[m][:])

        def plain_group(out, m, s, weights, bias_cols):
            with_bias = m < VB
            for e in range(K_TILES_H):
                nc.tensor.matmul(
                    out,
                    lhsT=hc_t[:, m, s, :].bitcast(BF16)[:, e::2],
                    rhs=weights[:, e, :],
                    start=(e == 0),
                    stop=(e == K_TILES_H - 1 and not with_bias),
                )
            if with_bias:
                nc.tensor.matmul(out, lhsT=ones[:, 0:P], rhs=bias_row[:, bias_cols], start=False, stop=True)

        def plain_og(m):
            plain_bank[m, 1] = psum.tile([P, BANK], F32, name="og", tag="bank")
            plain_group(plain_bank[m, 1][:], m, 0, whh[:, :, H:IH_COLS], slice(BANK, GATE_COLS))

        def plain_ai(m):
            plain_bank[m, 0] = psum.tile([P, BANK], F32, name="ai", tag="bank")
            plain_group(plain_bank[m, 0][:, H:BANK], m, 0, whh[:, :, 0:H], slice(H, BANK))
            plain_group(plain_bank[m, 0][:, 0:H], m, 1, awhh, slice(0, H))

        def warm_up():
            bank = psum.tile([P, BANK], F32, name="warm_bank", tag="bank")
            for cols in WARM:
                nc.tensor.matmul(bank[:, 0:cols], lhsT=ones[:, 0:P], rhs=ones[:, 0:cols], start=True, stop=True)

        def spread_bias(n):
            cols = slice(n * BANK, (n + 1) * BANK)
            bank = psum.tile([P, BANK], F32, name="bias_bank", tag="bank")
            nc.tensor.matmul(bank[:], lhsT=ones[:, 0:P], rhs=bias_row[:, cols], start=True, stop=True)
            nc.scalar.copy(out=bias_full[:, cols], in_=bank[:])

        def copy_plain(m, n):
            cols = slice(n * BANK, (n + 1) * BANK)
            if m < VB:
                nc.scalar.copy(out=plain[m][:, cols], in_=plain_bank[m, n][:])
            else:
                nc.vector.tensor_tensor(out=plain[m][:, cols], in0=plain_bank[m, n][:], in1=bias_full[:, cols], op=ALU.add)

        def regroup(dst, src):
            nc.vector.tensor_copy(
                out=dst.rearrange("p (c i t) -> p c t i", i=RUN, t=PACK),
                in_=src.rearrange("p (t c i) -> p c t i", t=PACK, i=RUN),
            )

        def regroup_al(g):
            grouped_w[g] = stage.tile([P, GATE_COLS * PACK], BF16, name="grouped_w", align_bytes=64, bufs=2)
            regroup(grouped_w[g][:, 0 : H * PACK], raw_al[g][:])

        def regroup_ih(g):
            regroup(grouped_w[g][:, H * PACK :], raw_ih[g][:])

        def regroup_ih_part(g, cols):
            dst = grouped_w[g][:, (H + cols.start) * PACK : (H + cols.stop) * PACK]
            nc.vector.tensor_copy(
                out=dst.rearrange("p (c i t) -> p c t i", i=RUN, t=PACK),
                in_=raw_ih[g][:].rearrange("p (t c) -> p t c", t=PACK)[:, :, cols].rearrange("p t (c i) -> p c t i", i=RUN),
            )

        def quantise_w(g, cols=slice(0, GATE_COLS)):
            nc.vector.quantize_mx(
                out=w_codes[g][:, cols].bitcast(FP8X4),
                scales=w_scales[g][:, cols],
                in_=grouped_w[g][:, cols.start * PACK : cols.stop * PACK],
            )

        def transpose_x(m):
            x_words = x_rows[m][:].bitcast(F32)
            x_bank[m] = []
            for b in range(PASSES // 2):
                bank = psum.tile([P, 4, P], F32, name="x_bank", tag="bank")
                for j in range(4):
                    g, u = 2 * b + j // 2, j % 2
                    nc.tensor.transpose(
                        bank[:, j, :], x_words[:, 2 * P * g + u : 2 * P * (g + 1) : 2], ident_f32[:]
                    )
                x_bank[m].append(bank)

        def open_x(m):
            grouped_x[m] = stage.tile([P, PASSES * P * PACK], BF16, name="grouped_x", align_bytes=64)

        def copy_x(m):
            open_x(m)
            words = grouped_x[m][:].bitcast(F32).rearrange("p (g r u) -> p g r u", g=PASSES, u=2)
            for b in range(PASSES // 2):
                nc.scalar.copy(
                    out=words[:, 2 * b : 2 * b + 2, :, :],
                    in_=x_bank[m][b][:].rearrange("p (g u) r -> p g r u", u=2),
                )

        def quantise_x(m):
            nc.vector.quantize_mx(out=x_codes[m][:].bitcast(FP8X4), scales=x_scales[m][:], in_=grouped_x[m][:])

        def mx_group(m, out, cols):
                for g in range(PASSES):
                    nc.tensor.matmul_mx(
                        out=out,
                        lhsT=x_codes[m][:, g * P : (g + 1) * P].bitcast(FP8X4),
                        lhsT_scale=x_scales[m][:, g * P : (g + 1) * P],
                        rhs=w_codes[g][:, cols].bitcast(FP8X4),
                        rhs_scale=w_scales[g][:, cols],
                        start=(g == 0),
                        stop=(g == PASSES - 1),
                    )

        def mx_matmuls(m):
            mx_bank[m] = [psum.tile([P, BANK], F32, name="mx_bank%d" % n, tag="bank") for n in range(HALVES)]
            mx_group(m, mx_bank[m][0][:], slice(0, BANK))
            if m < ROW_TILES - 1:
                mx_group(m, mx_bank[m][1][:], slice(BANK, GATE_COLS))
            else:
                mx_group(m, mx_bank[m][1][:, H:BANK], slice(BANK + H, GATE_COLS))
                mx_group(m, mx_bank[m][1][:, 0:H], slice(BANK, BANK + H))

        def add_plain(m, n, part=slice(0, BANK)):
            if n == 0:
                gates[m] = work.tile([P, GATE_COLS], F32, name="gates")
                w_i[m] = work.tile([P, H], F32, name="w_i")
                mix[m] = work.tile([P, H], F32, name="mix")
                tanh_c1[m] = work.tile([P, H], F32, name="tanh_c1")
            cols = slice(n * BANK + part.start, n * BANK + part.stop)
            nc.vector.tensor_tensor(out=gates[m][:, cols], in0=mx_bank[m][n][:, part], in1=plain[m][:, cols], op=ALU.add)

        def activate(m, func, cols):
            nc.scalar.activation(out=gates[m][:, cols], in_=gates[m][:, cols], func=func)

        def activate_alpha_i(m):
            activate(m, ACT.Sigmoid, slice(0, BANK))

        def activate_o(m):
            activate(m, ACT.Sigmoid, slice(BANK, BANK + H))

        def activate_g(m):
            activate(m, ACT.Tanh, slice(BANK + H, GATE_COLS))

        def gate_difference(m, lo=0, hi=H):
            nc.vector.tensor_tensor(
                out=w_i[m][:, lo:hi], in0=gates[m][:, H + lo : H + hi], in1=gates[m][:, lo:hi], op=ALU.subtract
            )

        def softmax_weight(m, lo=0, hi=H):
            nc.scalar.activation(out=w_i[m][:, lo:hi], in_=w_i[m][:, lo:hi], func=ACT.Sigmoid)

        def cell_difference(m):
            nc.vector.tensor_tensor(out=mix[m][:], in0=gates[m][:, BANK + H :], in1=c_rows[:, m, :], op=ALU.subtract)

        def weigh_difference(m, lo=0, hi=H):
            nc.vector.tensor_tensor(out=mix[m][:, lo:hi], in0=mix[m][:, lo:hi], in1=w_i[m][:, lo:hi], op=ALU.mult)

        def new_cell(m, lo=0, hi=H):
            nc.vector.tensor_tensor(
                out=c1_all[:, m, lo:hi], in0=mix[m][:, lo:hi], in1=c_rows[:, m, lo:hi], op=ALU.add
            )

        def tanh_cell(m, lo=0, hi=H):
            nc.scalar.activation(out=tanh_c1[m][:, lo:hi], in_=c1_all[:, m, lo:hi], func=ACT.Tanh)

        def new_hidden(m, lo=0, hi=H):
            nc.vector.tensor_tensor(
                out=h1_all[:, m, lo:hi], in0=gates[m][:, BANK + lo : BANK + hi], in1=tanh_c1[m][:, lo:hi], op=ALU.mult
            )

        def store(view, rows, first, count):
            nc.sync.dma_start(out=view[:, first : first + count, :], in_=rows[:, first : first + count, :])

        warm_up()
        for m in range(half):
            transpose_hidden(m, 0, h_rows)
            copy_hidden(m, 0)
        regroup_al(0)
        regroup_ih_part(0, i_cols)
        regroup_ih_part(0, og_cols)
        quantise_w(0)
        for m in range(half):
            plain_og(m)
            if m == half - 1:
                for j in range(half):
                    transpose_hidden(j, 1, c_rows)
                    copy_hidden(j, 1)
            copy_plain(m, 1)
        regroup_al(1)
        regroup_ih(1)
        for m in range(half):
            plain_ai(m)
            copy_plain(m, 0)
        regroup_al(2)
        quantise_w(1)
        regroup_ih(2)
        spread_bias(0)
        spread_bias(1)
        for m in range(half, ROW_TILES):
            transpose_both(m)
            copy_both(m)
        plain_og(4)
        copy_plain(4, 1)
        plain_ai(4)
        copy_plain(4, 0)
        plain_og(5)
        copy_plain(5, 1)
        plain_ai(5)
        copy_plain(5, 0)
        plain_og(6)
        plain_ai(6)
        transpose_x(0)
        copy_x(0)
        plain_og(7)
        plain_ai(7)
        transpose_x(1)
        copy_x(1)
        transpose_x(2)
        copy_x(2)
        regroup_al(3)
        quantise_w(2)
        regroup_ih(3)
        quantise_w(3)
        quantise_x(0)
        copy_plain(6, 1)
        copy_plain(6, 0)
        quantise_x(1)
        copy_plain(7, 1)
        copy_plain(7, 0)


        last = ROW_TILES - 1
        for m in range(last):
            mx_matmuls(m)
            if m + 3 < ROW_TILES:
                transpose_x(m + 3)
            if m == last - 1:
                mx_matmuls(last)
            add_plain(m, 0)
            activate_alpha_i(m)
            if m > 0:
                weigh_difference(m - 1)
            add_plain(m, 1)
            activate_g(m)
            activate_o(m)
            if m > 0:
                new_cell(m - 1)
                tanh_cell(m - 1)
                if m % 2 == 0:
                    store(c1_view, c1_all, m - 2, 2)
            if m + 2 < ROW_TILES:
                quantise_x(m + 2)
            if m == last - 1:
                add_plain(last, 0)
                activate_alpha_i(last)
            gate_difference(m)
            softmax_weight(m)
            cell_difference(m)
            if m + 3 < ROW_TILES:
                copy_x(m + 3)
            if m < last - 1 and m > 0:
                new_hidden(m - 1)
                if m % 2 == 0:
                    store(h1_view, h1_all, m - 2, 2)
        add_plain(last, 1, slice(H, BANK))
        activate_g(last)
        new_hidden(last - 2)
        store(h1_view, h1_all, last - 3, 2)
        gate_difference(last, 0, P)
        softmax_weight(last, 0, P)
        gate_difference(last, P, H)
        softmax_weight(last, P, H)
        weigh_difference(last - 1)
        cell_difference(last)
        new_cell(last - 1)
        weigh_difference(last, 0, P)
        tanh_cell(last - 1)
        weigh_difference(last, P, H)
        store(c1_view, c1_all, last - 1, 1)
        add_plain(last, 1, slice(0, H))
        activate_o(last)
        new_cell(last, 0, P)
        new_cell(last, P, H)
        tanh_cell(last, 0, P)
        tanh_cell(last, P, H)
        store(c1_view, c1_all, last, 1)
        new_hidden(last - 1)
        store(h1_view, h1_all, last - 1, 1)
        new_hidden(last, 0, P)
        new_hidden(last, P, H)
        store(h1_view, h1_all, last, 1)
